import numpy as np
import ml_dtypes


def mxq(x, axis, fmt="e4m3"):
    dtype, down = {"e4m3": (ml_dtypes.float8_e4m3fn, 7), "e5m2": (ml_dtypes.float8_e5m2, 14)}[fmt]
    v = np.moveaxis(np.asarray(x, np.float32).astype(ml_dtypes.bfloat16).astype(np.float64), axis, -1)
    blocks = v.reshape(v.shape[:-1] + (-1, 32))
    amax = np.abs(blocks).max(-1, keepdims=True)
    byte = np.maximum(np.where(amax > 0, np.frexp(amax)[1] - 1 + 127, 0) - down, 1)
    scale = np.exp2(byte - 127.0)
    codes = (blocks / scale).astype(np.float32).astype(dtype).astype(np.float64)
    return np.moveaxis((codes * scale).reshape(v.shape), -1, axis)


WIDE = False


def mx_kscale(k):
    if not WIDE:
        return np.ones(k)
    levels = np.array([10, -10, 5, -5, 0])
    a = np.random.permutation(np.resize(levels, k // 512 * 4)).reshape(k // 512, 4)
    idx = np.arange(k)
    return np.exp2(a[idx // 512, idx % 128 // 32])


BF16 = ml_dtypes.bfloat16


def bf(x):
    return np.asarray(x, np.float32).astype(BF16)


def f64(x):
    return np.asarray(x).astype(np.float64)


E2M1 = np.array([0.0, 0.5, 1.0, 1.5, 2.0, 3.0, 4.0, 6.0, -0.0, -0.5, -1.0, -1.5, -2.0, -3.0, -4.0, -6.0])


def pack_weight(w, fmt):
    k, n = w.shape
    w = f64(bf(w)).reshape(k // 32, 32, n)
    amax = np.abs(w).max(1)
    if fmt == "e4m3":
        byte = np.frexp(amax)[1] - 1 + 127 - 7
    else:
        mant, ex = np.frexp(amax / 6.0)
        byte = np.where(mant > 0.5, ex, ex - 1) + 127
    byte = np.clip(np.where(amax > 0, byte, 1), 1, 254)
    scaled = (w * np.exp2(127.0 - byte)[:, None, :]).reshape(k, n).astype(np.float32)
    by_word = np.ascontiguousarray(scaled.reshape(k // 512, 128, 4, n).transpose(0, 1, 3, 2))
    if fmt == "e4m3":
        words = by_word.astype(ml_dtypes.float8_e4m3fn).view(np.uint8)
    else:
        c = by_word.astype(ml_dtypes.float4_e2m1fn).view(np.uint8) & 0xF
        words = c[..., 0::2] | (c[..., 1::2] << 4)
    return np.ascontiguousarray(words), np.ascontiguousarray(byte.astype(np.uint8).reshape(k // 512, 16, n))


def unpack_weight(words, scales, fmt):
    g, p, n, _ = words.shape
    if fmt == "e4m3":
        vals = np.ascontiguousarray(words).view(ml_dtypes.float8_e4m3fn).astype(np.float64)
    else:
        nib = np.empty((g, p, n, 4), np.uint8)
        nib[..., 0::2] = words & 0xF
        nib[..., 1::2] = words >> 4
        vals = E2M1[nib]
    vals = vals * np.repeat(np.exp2(scales.astype(np.float64) - 127.0), 8, axis=1)[..., None]
    return vals.transpose(0, 1, 3, 2).reshape(g * 512, n)


B, L, D, NK = 1, 128, 2048, 2048
Q = 0.25 * np.sqrt(D)


def setup_inputs():
    t = mx_kscale(NK)
    f = t / t.max()
    ls = bf(np.log(2.0) * (1.0 + 0.1 * np.random.standard_normal(D)))
    x = np.random.standard_normal((B, L, D)) * np.sqrt(Q / D) * f64(ls)
    g = np.random.standard_normal((NK, D)) * np.sqrt(Q / D)
    g = g * np.sqrt(1.0 - 2.0 * np.log(f) / np.sum(g * g, axis=1))[:, None]
    w = np.random.standard_normal((D, NK)) * np.exp(Q) / np.sqrt(NK) / f
    words, scales = pack_weight(np.ascontiguousarray(w.T), "e4m3")
    return {"x": bf(x), "centers": bf(g * f64(ls)), "lengthscale": ls,
            "W_out_words": words, "W_out_scales": scales, "b_out": bf(np.random.standard_normal(D) * 0.3)}


def reference(x, centers, lengthscale, W_out_words, W_out_scales, b_out):
    b, l, d = x.shape
    xs = f64(x).reshape(b * l, d) / f64(lengthscale)
    cs = f64(centers) / f64(lengthscale)
    cross = mxq(xs, 1, "e4m3") @ mxq(cs, 1, "e4m3").T
    sq = (np.sum(xs * xs, axis=-1)[:, None]
          + np.sum(cs * cs, axis=-1)[None, :]
          - 2.0 * cross)
    K = np.exp(-0.5 * np.maximum(sq, 0.0))
    out = (mxq(K, 1, "e4m3") @ unpack_weight(W_out_words, W_out_scales, "e4m3")) + f64(b_out)
    return out.reshape(b, l, d)

@@ -1,0 +1,299 @@
+from contextlib import ExitStack
+
+import concourse.bass as bass
+import concourse.mybir as mybir
+import concourse.tile as tile
+from concourse.masks import make_identity
+
+F32 = mybir.dt.float32
+BF16 = mybir.dt.bfloat16
+U8 = mybir.dt.uint8
+U32 = mybir.dt.uint32
+I32 = mybir.dt.int32
+FP8X4 = mybir.dt.float8_e4m3fn_x4
+ACT = mybir.ActivationFunctionType
+ALU = mybir.AluOpType
+
+P = 128
+D = 2048
+NK = 2048
+TILES = 17
+FLOPS = 2 * 128 * 2048 * 2048 * 2
+
+VECTOR_NATURAL = (1, 3, 7, 11, 15)
+VECTOR_STEPS = (2, 4, 7, 10, 13)
+G_CHUNK = 512
+
+
+def tile_gpytorchrbfkernelffn_w_kernel(tc, x, centers, lengthscale, W_out_words, W_out_scales, b_out, out):
+    nc = tc.nc
+    with ExitStack() as ctx:
+        ctx.enter_context(tc.manual_schedule())
+        keep = ctx.enter_context(tc.tile_pool(name="keep", bufs=1))
+        work = ctx.enter_context(tc.tile_pool(name="work", bufs=2))
+        ring = ctx.enter_context(tc.tile_pool(name="ring", bufs=3))
+        ps_t = ctx.enter_context(tc.psum_pool(name="ps_t", bufs=4))
+        ps_z = ctx.enter_context(tc.psum_pool(name="ps_z", bufs=2))
+        ps_m = ctx.enter_context(tc.psum_pool(name="ps_m", bufs=1))
+
+        tab = keep.tile([P, 256], BF16)
+        nc.vector.memset(tab[:], 0.0)
+        planes = keep.tile([P, NK], U8, align_bytes=64)
+        nc.vector.memset(planes[:].bitcast(I32), 0)
+        warm = keep.tile([P, 1], F32)
+        nc.vector.memset(warm[:], 0.0)
+        warm2 = keep.tile([P, 1], F32)
+        nc.scalar.activation(out=warm2[:], in_=warm[:], func=ACT.Exp)
+        ident = keep.tile([P, P], F32)
+        make_identity(nc, ident[:])
+
+        nc.sync.dma_start(out=tab[0:8, :], in_=lengthscale.rearrange("(w q) -> w q", q=256))
+        nat = []
+        x_nat = keep.tile([P, D], BF16)
+        nc.sync.dma_start(out=x_nat[:], in_=x.rearrange("b l d -> (b l) d"))
+        nat.append(x_nat)
+        c_view = centers.rearrange("(g p t) d -> g p t d", p=P, t=4)
+        for n in range(1, TILES):
+            c_nat = keep.tile([P, D], BF16, name="c_nat%d" % n)
+            nc.sync.dma_start(out=c_nat[:], in_=c_view[(n - 1) // 4, :, (n - 1) % 4, :])
+            nat.append(c_nat)
+        for q in range(4):
+            nc.sync.dma_start(
+                out=planes[32 * q : 32 * q + 16, :].bitcast(I32),
+                in_=W_out_scales[:, 4 * q : 4 * q + 4, :].bitcast(I32),
+            )
+        w_words = []
+        for g in range(4):
+            ww = keep.tile([P, 4 * NK], U8, name="w_words%d" % g, align_bytes=64)
+            nc.sync.dma_start(out=ww[:].bitcast(I32), in_=W_out_words[g].rearrange("p n t -> p (n t)").bitcast(I32))
+            w_words.append(ww)
+        bias_b = keep.tile([P, NK], BF16)
+        nc.sync.dma_start(out=bias_b[:], in_=b_out.partition_broadcast(P))
+
+        ls_t = keep.tile([P, 16], F32)
+        rls_t = keep.tile([P, 16], F32)
+        rls_b = keep.tile([P, D], F32)
+        csq = keep.tile([P, TILES], F32)
+        nh = keep.tile([P, TILES], F32)
+        nhx_b = keep.tile([P, P], F32)
+        junk = keep.tile([P, D], BF16)
+        x_codes = keep.tile([P, 512], U32, align_bytes=64)
+        x_plane = keep.tile([P, 512], U8, align_bytes=64)
+        k_codes = keep.tile([P, 4, P], U32, align_bytes=64)
+        k_plane = keep.tile([P, 4, P], U8, align_bytes=64)
+
+        tab_t = ps_m.tile([P, 512], F32, tag="m")
+        nc.tensor.transpose(tab_t[:, 0:P], tab[:].bitcast(F32), ident[:])
+        nc.vector.tensor_copy(out=ls_t[:], in_=tab_t[:, 0:8].bitcast(BF16))
+        nc.vector.reciprocal(out=rls_t[:], in_=ls_t[:])
+
+        banks = {}
+        grouped = {}
+        codes = {}
+        z_bank = {}
+        wide = {}
+        z1s = {}
+        exps = {}
+        kgs = {}
+
+        def transposes(n):
+            words = nat[n][:].bitcast(F32)
+            for h in range(2):
+                tb = ps_t.tile([P, 2, 2, P], F32, tag="t", name="tb")
+                for u in range(2):
+                    for gg in range(2):
+                        w = 2 * (2 * h + gg) + u
+                        nc.tensor.transpose(tb[:, u, gg, :], words[:, P * w : P * w + P], ident[:])
+                banks[(n, h)] = tb
+
+        def spread_rls(b):
+            pb = ps_z.tile([P, 4, P], F32, tag="z", name="pb")
+            for k in range(4):
+                nc.tensor.transpose(pb[:, k, :], rls_t[:, 4 * b + k : 4 * b + k + 1].to_broadcast([P, P]), ident[:])
+            nc.scalar.copy(
+                out=rls_b[:, 512 * b : 512 * b + 512].rearrange("p (u q e) -> p u q e", u=2, q=P, e=2),
+                in_=pb[:].rearrange("p (u e) q -> p u q e", u=2, e=2),
+            )
+
+        def scale_out(n):
+            gr = ring.tile([P, 4, P, 4], BF16, tag="grouped", name="gr", align_bytes=64)
+            grouped[n] = gr
+            for h in range(2):
+                tb = banks[(n, h)]
+                nc.vector.tensor_tensor(
+                    out=gr[:, 2 * h : 2 * h + 2, :, :].rearrange("p g j (u e) -> p g j u e", u=2, e=2),
+                    in0=tb[:]
+                    .rearrange("p u g j -> p (u g j)")
+                    .bitcast(BF16)
+                    .rearrange("p (u g j e) -> p g j u e", u=2, g=2, j=P, e=2),
+                    in1=rls_t[:, 8 * h : 8 * h + 8]
+                    .rearrange("p (g u e) -> p g u e", g=2, u=2, e=2)
+                    .unsqueeze(2)
+                    .to_broadcast([P, 2, P, 2, 2]),
+                    op=ALU.mult,
+                )
+
+        def quantise(n):
+            if n == 0:
+                cd, pl = x_codes, x_plane
+            else:
+                cd = ring.tile([P, 512], U32, tag="codes", name="cd", align_bytes=64)
+                pl = ring.tile([P, 512], U8, tag="plane", name="pl", align_bytes=64)
+            codes[n] = (cd, pl)
+            nc.vector.quantize_mx(
+                out=cd[:].bitcast(FP8X4), scales=pl[:], in_=grouped[n][:].rearrange("p g j t -> p (g j t)")
+            )
+
+        def stage1(n):
+            g, t = (n - 1) // 4, (n - 1) % 4
+            if t == 0:
+                z_bank[g] = ps_z.tile([P, 4, P], F32, tag="z", name="zb")
+            cd, pl = codes[n]
+            for c in range(4):
+                cols = slice(P * c, P * c + P)
+                nc.tensor.matmul_mx(
+                    out=z_bank[g][:, t, :],
+                    lhsT=cd[:, cols].bitcast(FP8X4),
+                    lhsT_scale=pl[:, cols],
+                    rhs=x_codes[:, cols].bitcast(FP8X4),
+                    rhs_scale=x_plane[:, cols],
+                    start=(c == 0),
+                    stop=(c == 3),
+                )
+
+        def natural_multiply(n):
+            if n in VECTOR_NATURAL:
+                w = work.tile([P, D], F32, tag="wv", name="wv", bufs=1)
+                nc.vector.tensor_tensor(out=w[:], in0=nat[n][:], in1=rls_b[:], op=ALU.mult)
+            else:
+                w = work.tile([P, D], F32, tag="wg", name="wg")
+                for c0 in range(0, D, G_CHUNK):
+                    cols = slice(c0, c0 + G_CHUNK)
+                    nc.gpsimd.tensor_tensor(out=w[:, cols], in0=nat[n][:, cols], in1=rls_b[:, cols], op=ALU.mult)
+            wide[n] = w
+
+        def square_sum(n):
+            nc.scalar.activation(out=junk[:], in_=wide[n][:], func=ACT.Square, accum_out=csq[:, n : n + 1])
+
+        def halve(lo, hi):
+            nc.scalar.mul(out=nh[:, lo:hi], in_=csq[:, lo:hi], mul=-0.5)
+
+        def add_xsq(g):
+            z1 = work.tile([P, 4, P], F32, tag="z1", name="z1")
+            nc.vector.tensor_tensor(
+                out=z1[:], in0=z_bank[g][:], in1=nhx_b[:].unsqueeze(1).to_broadcast([P, 4, P]), op=ALU.add
+            )
+            z1s[g] = z1
+
+        def exponentials(g):
+            ex = work.tile([P, 4, P], F32, tag="ex", name="ex")
+            for t in range(4):
+                n = 4 * g + t + 1
+                nc.scalar.activation(
+                    out=ex[:, t, :], in_=z1s[g][:, t, :], func=ACT.Exp, bias=nh[:, n : n + 1], scale=1.0
+                )
+            exps[g] = ex
+
+        def clamp(g):
+            kg = work.tile([P, P, 4], BF16, tag="kg", name="kg", align_bytes=64)
+            nc.vector.tensor_scalar(
+                out=kg[:], in0=exps[g][:].rearrange("p t i -> p i t"), scalar1=1.0, scalar2=None, op0=ALU.min
+            )
+            kgs[g] = kg
+
+        def quantise_k(g):
+            nc.vector.quantize_mx(
+                out=k_codes[:, g, :].bitcast(FP8X4), scales=k_plane[:, g, :], in_=kgs[g][:].rearrange("p i t -> p (i t)")
+            )
+
+        events = {}
+
+        def at(step, where, fn, arg):
+            key = (step, where)
+            if key not in events:
+                events[key] = []
+            events[key].append((fn, arg))
+
+        def run(step, where):
+            for fn, arg in events.get((step, where), []):
+                fn(arg)
+
+        g_list = [n for n in range(TILES) if n not in VECTOR_NATURAL]
+        sq_step = {}
+        for k, n in enumerate(g_list):
+            sq_step[k] = 3 + k + (k + 3) // 5
+            at(sq_step[k], "early", square_sum, n)
+            if k + 2 < len(g_list):
+                at(sq_step[k], "early", natural_multiply, g_list[k + 2])
+        for n, step in zip(VECTOR_NATURAL, VECTOR_STEPS):
+            at(step, "mid", natural_multiply, n)
+            at(step + 1, "early", square_sum, n)
+
+        def spread_xsq(unused):
+            halve(0, 1)
+            pm = ps_m.tile([P, 512], F32, tag="m", name="pm")
+            nc.tensor.transpose(pm[:, 0:P], nh[:, 0:1].to_broadcast([P, P]), ident[:])
+            banks["xsq"] = pm
+
+        def copy_xsq(unused):
+            nc.vector.tensor_copy(out=nhx_b[:], in_=banks["xsq"][:, 0:P])
+
+        at(5, "late", spread_xsq, 0)
+        at(6, "early", copy_xsq, 0)
+        for g in range(3):
+            at(4 * g + 6, "mid", add_xsq, g)
+            at(4 * g + 6, "mid", lambda gg: halve(4 * gg + 1, 4 * gg + 5), g)
+            at(4 * g + 6, "mid", exponentials, g)
+            at(4 * g + 7, "early", clamp, g)
+            at(4 * g + 7, "mid", quantise_k, g)
+
+        transposes(0)
+        for b in range(4):
+            spread_rls(b)
+        natural_multiply(g_list[0])
+        natural_multiply(g_list[1])
+        for s in range(TILES):
+            if s + 1 < TILES:
+                transposes(s + 1)
+            run(s, "early")
+            scale_out(s)
+            if s >= 1:
+                quantise(s - 1)
+            if s >= 2:
+                stage1(s - 1)
+            run(s, "mid")
+            run(s, "late")
+
+        quantise(16)
+        stage1(16)
+        accs = []
+        for c in range(4):
+            acc = ps_t.tile([P, 512], F32, tag="t", name="acc")
+            accs.append(acc)
+
+        def stage2(g, c):
+            nc.tensor.matmul_mx(
+                out=accs[c][:],
+                lhsT=k_codes[:, g, :].bitcast(FP8X4),
+                lhsT_scale=k_plane[:, g, :],
+                rhs=w_words[g][:, 2048 * c : 2048 * c + 2048].bitcast(FP8X4),
+                rhs_scale=planes[4 * g : P, 512 * c : 512 * c + 512],
+                start=(g == 0),
+                stop=(g == 3),
+            )
+
+        for c in range(4):
+            for g in range(3):
+                stage2(g, c)
+        add_xsq(3)
+        halve(13, 17)
+        exponentials(3)
+        clamp(3)
+        quantise_k(3)
+        out_rows = out.rearrange("b l n -> (b l) n")
+        for c in range(4):
+            stage2(3, c)
+            res = work.tile([P, 512], F32, tag="res", name="res", bufs=4)
+            cols = slice(512 * c, 512 * c + 512)
+            nc.vector.tensor_tensor(out=res[:], in0=accs[c][:], in1=bias_b[:, cols], op=ALU.add)
+            nc.sync.dma_start(out=out_rows[:, cols], in_=res[:])

@@ -1,8 +1,6 @@
 from contextlib import ExitStack
 
-import concourse.bass as bass
 import concourse.mybir as mybir
-import concourse.tile as tile
 from concourse.masks import make_identity
 
 F32 = mybir.dt.float32
@@ -20,10 +18,6 @@ NK = 2048
 TILES = 17
 FLOPS = 2 * 128 * 2048 * 2048 * 2
 
-VECTOR_NATURAL = (1, 3, 7, 11, 15)
-VECTOR_STEPS = (2, 4, 7, 10, 13)
-G_CHUNK = 512
-
 
 def tile_gpytorchrbfkernelffn_w_kernel(tc, x, centers, lengthscale, W_out_words, W_out_scales, b_out, out):
     nc = tc.nc
@@ -34,7 +28,7 @@ def tile_gpytorchrbfkernelffn_w_kernel(tc, x, centers, lengthscale, W_out_words,
         ring = ctx.enter_context(tc.tile_pool(name="ring", bufs=3))
         ps_t = ctx.enter_context(tc.psum_pool(name="ps_t", bufs=4))
         ps_z = ctx.enter_context(tc.psum_pool(name="ps_z", bufs=2))
-        ps_m = ctx.enter_context(tc.psum_pool(name="ps_m", bufs=1))
+        ps_r = ctx.enter_context(tc.psum_pool(name="ps_r", bufs=2))
 
         tab = keep.tile([P, 256], BF16)
         nc.vector.memset(tab[:], 0.0)
@@ -72,26 +66,26 @@ def tile_gpytorchrbfkernelffn_w_kernel(tc, x, centers, lengthscale, W_out_words,
 
         ls_t = keep.tile([P, 16], F32)
         rls_t = keep.tile([P, 16], F32)
-        rls_b = keep.tile([P, D], F32)
         csq = keep.tile([P, TILES], F32)
         nh = keep.tile([P, TILES], F32)
         nhx_b = keep.tile([P, P], F32)
-        junk = keep.tile([P, D], BF16)
+        junk = keep.tile([P, P], F32)
         x_codes = keep.tile([P, 512], U32, align_bytes=64)
         x_plane = keep.tile([P, 512], U8, align_bytes=64)
         k_codes = keep.tile([P, 4, P], U32, align_bytes=64)
         k_plane = keep.tile([P, 4, P], U8, align_bytes=64)
 
-        tab_t = ps_m.tile([P, 512], F32, tag="m")
+        tab_t = ps_r.tile([P, 512], F32, tag="r")
         nc.tensor.transpose(tab_t[:, 0:P], tab[:].bitcast(F32), ident[:])
         nc.vector.tensor_copy(out=ls_t[:], in_=tab_t[:, 0:8].bitcast(BF16))
         nc.vector.reciprocal(out=rls_t[:], in_=ls_t[:])
 
         banks = {}
+        squared = {}
+        sums = {}
         grouped = {}
         codes = {}
         z_bank = {}
-        wide = {}
         z1s = {}
         exps = {}
         kgs = {}
@@ -106,32 +100,58 @@ def tile_gpytorchrbfkernelffn_w_kernel(tc, x, centers, lengthscale, W_out_words,
                         nc.tensor.transpose(tb[:, u, gg, :], words[:, P * w : P * w + P], ident[:])
                 banks[(n, h)] = tb
 
-        def spread_rls(b):
-            pb = ps_z.tile([P, 4, P], F32, tag="z", name="pb")
-            for k in range(4):
-                nc.tensor.transpose(pb[:, k, :], rls_t[:, 4 * b + k : 4 * b + k + 1].to_broadcast([P, P]), ident[:])
-            nc.scalar.copy(
-                out=rls_b[:, 512 * b : 512 * b + 512].rearrange("p (u q e) -> p u q e", u=2, q=P, e=2),
-                in_=pb[:].rearrange("p (u e) q -> p u q e", u=2, e=2),
+        def squares(n, h):
+            sq = ring.tile([P, 8, P], F32, tag="sq", name="sq", bufs=4)
+            view = (
+                banks[(n, h)][:]
+                .rearrange("p u g j -> p (u g j)")
+                .bitcast(BF16)
+                .rearrange("p (u g j e) -> p u g e j", u=2, g=2, j=P, e=2)
             )
+            for u in range(2):
+                for gg in range(2):
+                    for e in range(2):
+                        c = 4 * (2 * h + gg) + 2 * u + e
+                        nc.scalar.activation(
+                            out=sq[:, 4 * u + 2 * gg + e, :],
+                            in_=view[:, u, gg, e, :],
+                            func=ACT.Square,
+                            scale=rls_t[:, c : c + 1],
+                        )
+            squared[(n, h)] = sq
 
-        def scale_out(n):
-            gr = ring.tile([P, 4, P, 4], BF16, tag="grouped", name="gr", align_bytes=64)
-            grouped[n] = gr
+        def sum_over_d(n):
+            rt = ps_r.tile([P, 512], F32, tag="r", name="rt")
             for h in range(2):
-                tb = banks[(n, h)]
-                nc.vector.tensor_tensor(
-                    out=gr[:, 2 * h : 2 * h + 2, :, :].rearrange("p g j (u e) -> p g j u e", u=2, e=2),
-                    in0=tb[:]
-                    .rearrange("p u g j -> p (u g j)")
-                    .bitcast(BF16)
-                    .rearrange("p (u g j e) -> p g j u e", u=2, g=2, j=P, e=2),
-                    in1=rls_t[:, 8 * h : 8 * h + 8]
-                    .rearrange("p (g u e) -> p g u e", g=2, u=2, e=2)
-                    .unsqueeze(2)
-                    .to_broadcast([P, 2, P, 2, 2]),
-                    op=ALU.mult,
-                )
+                for k in range(8):
+                    nc.tensor.matmul(
+                        out=rt[:, 0:P],
+                        lhsT=squared[(n, h)][:, k, :],
+                        rhs=ident[:],
+                        is_transpose=True,
+                        start=(h == 0 and k == 0),
+                        stop=(h == 1 and k == 7),
+                    )
+            sums[n] = rt
+
+        def reduce_sum(n):
+            nc.scalar.activation(out=junk[:], in_=sums[n][:, 0:P], func=ACT.Copy, accum_out=csq[:, n : n + 1])
+
+        def scale_bank(n, h):
+            if n not in grouped:
+                grouped[n] = ring.tile([P, 4, P, 4], BF16, tag="grouped", name="gr", align_bytes=64)
+            nc.vector.tensor_tensor(
+                out=grouped[n][:, 2 * h : 2 * h + 2, :, :].rearrange("p g j (u e) -> p g j u e", u=2, e=2),
+                in0=banks[(n, h)][:]
+                .rearrange("p u g j -> p (u g j)")
+                .bitcast(BF16)
+                .rearrange("p (u g j e) -> p g j u e", u=2, g=2, j=P, e=2),
+                in1=rls_t[:, 8 * h : 8 * h + 8]
+                .rearrange("p (g u e) -> p g u e", g=2, u=2, e=2)
+                .unsqueeze(2)
+                .to_broadcast([P, 2, P, 2, 2]),
+                op=ALU.mult,
+            )
 
         def quantise(n):
             if n == 0:
@@ -161,20 +181,6 @@ def tile_gpytorchrbfkernelffn_w_kernel(tc, x, centers, lengthscale, W_out_words,
                     stop=(c == 3),
                 )
 
-        def natural_multiply(n):
-            if n in VECTOR_NATURAL:
-                w = work.tile([P, D], F32, tag="wv", name="wv", bufs=1)
-                nc.vector.tensor_tensor(out=w[:], in0=nat[n][:], in1=rls_b[:], op=ALU.mult)
-            else:
-                w = work.tile([P, D], F32, tag="wg", name="wg")
-                for c0 in range(0, D, G_CHUNK):
-                    cols = slice(c0, c0 + G_CHUNK)
-                    nc.gpsimd.tensor_tensor(out=w[:, cols], in0=nat[n][:, cols], in1=rls_b[:, cols], op=ALU.mult)
-            wide[n] = w
-
-        def square_sum(n):
-            nc.scalar.activation(out=junk[:], in_=wide[n][:], func=ACT.Square, accum_out=csq[:, n : n + 1])
-
         def halve(lo, hi):
             nc.scalar.mul(out=nh[:, lo:hi], in_=csq[:, lo:hi], mul=-0.5)
 
@@ -186,6 +192,7 @@ def tile_gpytorchrbfkernelffn_w_kernel(tc, x, centers, lengthscale, W_out_words,
             z1s[g] = z1
 
         def exponentials(g):
+            halve(4 * g + 1, 4 * g + 5)
             ex = work.tile([P, 4, P], F32, tag="ex", name="ex")
             for t in range(4):
                 n = 4 * g + t + 1
@@ -206,6 +213,15 @@ def tile_gpytorchrbfkernelffn_w_kernel(tc, x, centers, lengthscale, W_out_words,
                 out=k_codes[:, g, :].bitcast(FP8X4), scales=k_plane[:, g, :], in_=kgs[g][:].rearrange("p i t -> p (i t)")
             )
 
+        def spread_xsq(unused):
+            halve(0, 1)
+            pm = ps_r.tile([P, 512], F32, tag="r", name="pm")
+            nc.tensor.transpose(pm[:, 0:P], nh[:, 0:1].to_broadcast([P, P]), ident[:])
+            banks["xsq"] = pm
+
+        def copy_xsq(unused):
+            nc.vector.tensor_copy(out=nhx_b[:], in_=banks["xsq"][:, 0:P])
+
         events = {}
 
         def at(step, where, fn, arg):
@@ -218,51 +234,42 @@ def tile_gpytorchrbfkernelffn_w_kernel(tc, x, centers, lengthscale, W_out_words,
             for fn, arg in events.get((step, where), []):
                 fn(arg)
 
-        g_list = [n for n in range(TILES) if n not in VECTOR_NATURAL]
-        sq_step = {}
-        for k, n in enumerate(g_list):
-            sq_step[k] = 3 + k + (k + 3) // 5
-            at(sq_step[k], "early", square_sum, n)
-            if k + 2 < len(g_list):
-                at(sq_step[k], "early", natural_multiply, g_list[k + 2])
-        for n, step in zip(VECTOR_NATURAL, VECTOR_STEPS):
-            at(step, "mid", natural_multiply, n)
-            at(step + 1, "early", square_sum, n)
-
-        def spread_xsq(unused):
-            halve(0, 1)
-            pm = ps_m.tile([P, 512], F32, tag="m", name="pm")
-            nc.tensor.transpose(pm[:, 0:P], nh[:, 0:1].to_broadcast([P, P]), ident[:])
-            banks["xsq"] = pm
-
-        def copy_xsq(unused):
-            nc.vector.tensor_copy(out=nhx_b[:], in_=banks["xsq"][:, 0:P])
-
-        at(5, "late", spread_xsq, 0)
-        at(6, "early", copy_xsq, 0)
+        at(1, "mid", spread_xsq, 0)
+        at(2, "early", copy_xsq, 0)
         for g in range(3):
             at(4 * g + 6, "mid", add_xsq, g)
-            at(4 * g + 6, "mid", lambda gg: halve(4 * gg + 1, 4 * gg + 5), g)
             at(4 * g + 6, "mid", exponentials, g)
             at(4 * g + 7, "early", clamp, g)
             at(4 * g + 7, "mid", quantise_k, g)
 
         transposes(0)
-        for b in range(4):
-            spread_rls(b)
-        natural_multiply(g_list[0])
-        natural_multiply(g_list[1])
+        transposes(1)
+        squares(0, 0)
+        scale_bank(0, 1)
+        scale_bank(0, 0)
+        squares(0, 1)
+        sum_over_d(0)
+        squares(1, 0)
+        squares(1, 1)
+        reduce_sum(0)
         for s in range(TILES):
             if s + 1 < TILES:
-                transposes(s + 1)
+                sum_over_d(s + 1)
             run(s, "early")
-            scale_out(s)
+            if s > 0:
+                scale_bank(s, 0)
+                scale_bank(s, 1)
+            if s + 2 < TILES:
+                transposes(s + 2)
+                squares(s + 2, 0)
+                squares(s + 2, 1)
+            if s + 1 < TILES:
+                reduce_sum(s + 1)
             if s >= 1:
                 quantise(s - 1)
             if s >= 2:
                 stage1(s - 1)
             run(s, "mid")
-            run(s, "late")
 
         quantise(16)
         stage1(16)
@@ -286,7 +293,6 @@ def tile_gpytorchrbfkernelffn_w_kernel(tc, x, centers, lengthscale, W_out_words,
             for g in range(3):
                 stage2(g, c)
         add_xsq(3)
-        halve(13, 17)
         exponentials(3)
         clamp(3)
         quantise_k(3)

@@ -17,6 +17,7 @@ D = 2048
 NK = 2048
 TILES = 17
 FLOPS = 2 * 128 * 2048 * 2048 * 2
+NATURAL = (4, 8, 12, 16)
 
 
 def tile_gpytorchrbfkernelffn_w_kernel(tc, x, centers, lengthscale, W_out_words, W_out_scales, b_out, out):
@@ -70,6 +71,9 @@ def tile_gpytorchrbfkernelffn_w_kernel(tc, x, centers, lengthscale, W_out_words,
         nh = keep.tile([P, TILES], F32)
         nhx_b = keep.tile([P, P], F32)
         junk = keep.tile([P, P], F32)
+        junk2 = keep.tile([P, D], BF16)
+        rls_b = keep.tile([P, D], F32)
+        wide = {}
         x_codes = keep.tile([P, 512], U32, align_bytes=64)
         x_plane = keep.tile([P, 512], U8, align_bytes=64)
         k_codes = keep.tile([P, 4, P], U32, align_bytes=64)
@@ -101,7 +105,7 @@ def tile_gpytorchrbfkernelffn_w_kernel(tc, x, centers, lengthscale, W_out_words,
                 banks[(n, h)] = tb
 
         def squares(n, h):
-            sq = ring.tile([P, 8, P], F32, tag="sq", name="sq", bufs=4)
+            sq = ring.tile([P, 8, P], F32, tag="sq", name="sq", bufs=6)
             view = (
                 banks[(n, h)][:]
                 .rearrange("p u g j -> p (u g j)")
@@ -120,19 +124,37 @@ def tile_gpytorchrbfkernelffn_w_kernel(tc, x, centers, lengthscale, W_out_words,
                         )
             squared[(n, h)] = sq
 
-        def sum_over_d(n):
-            rt = ps_r.tile([P, 512], F32, tag="r", name="rt")
-            for h in range(2):
-                for k in range(8):
-                    nc.tensor.matmul(
-                        out=rt[:, 0:P],
-                        lhsT=squared[(n, h)][:, k, :],
-                        rhs=ident[:],
-                        is_transpose=True,
-                        start=(h == 0 and k == 0),
-                        stop=(h == 1 and k == 7),
-                    )
-            sums[n] = rt
+        def sum_unit(n, h):
+            if h == 0:
+                sums[n] = ps_r.tile([P, 512], F32, tag="r", name="rt")
+            for k in range(8):
+                nc.tensor.matmul(
+                    out=sums[n][:, 0:P],
+                    lhsT=squared[(n, h)][:, k, :],
+                    rhs=ident[:],
+                    is_transpose=True,
+                    start=(h == 0 and k == 0),
+                    stop=(h == 1 and k == 7),
+                )
+
+        def spread_rls(b):
+            pb = ps_z.tile([P, 4, P], F32, tag="z", name="pb")
+            for k in range(4):
+                nc.tensor.transpose(pb[:, k, :], rls_t[:, 4 * b + k : 4 * b + k + 1].to_broadcast([P, P]), ident[:])
+            nc.scalar.copy(
+                out=rls_b[:, 512 * b : 512 * b + 512].rearrange("p (u q e) -> p u q e", u=2, q=P, e=2),
+                in_=pb[:].rearrange("p (u e) q -> p u q e", u=2, e=2),
+            )
+
+        def natural_chunk(arg):
+            n, c = arg
+            if c == 0:
+                wide[n] = work.tile([P, D], F32, tag="wv", name="wv")
+            cols = slice(512 * c, 512 * c + 512)
+            nc.vector.tensor_tensor(out=wide[n][:, cols], in0=nat[n][:, cols], in1=rls_b[:, cols], op=ALU.mult)
+
+        def square_sum(n):
+            nc.scalar.activation(out=junk2[:], in_=wide[n][:], func=ACT.Square, accum_out=csq[:, n : n + 1])
 
         def reduce_sum(n):
             nc.scalar.activation(out=junk[:], in_=sums[n][:, 0:P], func=ACT.Copy, accum_out=csq[:, n : n + 1])
@@ -215,7 +237,7 @@ def tile_gpytorchrbfkernelffn_w_kernel(tc, x, centers, lengthscale, W_out_words,
 
         def spread_xsq(unused):
             halve(0, 1)
-            pm = ps_r.tile([P, 512], F32, tag="r", name="pm")
+            pm = ps_z.tile([P, 512], F32, tag="z", name="pm")
             nc.tensor.transpose(pm[:, 0:P], nh[:, 0:1].to_broadcast([P, P]), ident[:])
             banks["xsq"] = pm
 
@@ -235,48 +257,23 @@ def tile_gpytorchrbfkernelffn_w_kernel(tc, x, centers, lengthscale, W_out_words,
                 fn(arg)
 
         at(1, "mid", spread_xsq, 0)
-        at(2, "early", copy_xsq, 0)
+        at(5, "early", copy_xsq, 0)
         for g in range(3):
             at(4 * g + 6, "mid", add_xsq, g)
             at(4 * g + 6, "mid", exponentials, g)
             at(4 * g + 7, "early", clamp, g)
             at(4 * g + 7, "mid", quantise_k, g)
+        for n in NATURAL:
+            for c in range(4):
+                at(n - 3 + c, "early", natural_chunk, (n, c))
+            if n < 16:
+                at(n + 1, "early", square_sum, n)
+            else:
+                at(n, "mid", square_sum, n)
 
-        transposes(0)
-        transposes(1)
-        squares(0, 0)
-        scale_bank(0, 1)
-        scale_bank(0, 0)
-        squares(0, 1)
-        sum_over_d(0)
-        squares(1, 0)
-        squares(1, 1)
-        reduce_sum(0)
-        for s in range(TILES):
-            if s + 1 < TILES:
-                sum_over_d(s + 1)
-            run(s, "early")
-            if s > 0:
-                scale_bank(s, 0)
-                scale_bank(s, 1)
-            if s + 2 < TILES:
-                transposes(s + 2)
-                squares(s + 2, 0)
-                squares(s + 2, 1)
-            if s + 1 < TILES:
-                reduce_sum(s + 1)
-            if s >= 1:
-                quantise(s - 1)
-            if s >= 2:
-                stage1(s - 1)
-            run(s, "mid")
-
-        quantise(16)
-        stage1(16)
+        units = [(n, h) for n in range(1, TILES) if n not in NATURAL for h in range(2)]
+        taken = 0
         accs = []
-        for c in range(4):
-            acc = ps_t.tile([P, 512], F32, tag="t", name="acc")
-            accs.append(acc)
 
         def stage2(g, c):
             nc.tensor.matmul_mx(
@@ -289,7 +286,61 @@ def tile_gpytorchrbfkernelffn_w_kernel(tc, x, centers, lengthscale, W_out_words,
                 stop=(g == 3),
             )
 
-        for c in range(4):
+        transposes(0)
+        transposes(1)
+        squares(0, 0)
+        scale_bank(0, 1)
+        scale_bank(0, 0)
+        squares(0, 1)
+        sum_unit(0, 0)
+        sum_unit(0, 1)
+        squares(1, 0)
+        squares(1, 1)
+        reduce_sum(0)
+        for s in range(TILES):
+            run(s, "early")
+            done = []
+            for k in range(2 - s % 2):
+                if taken < len(units):
+                    n, h = units[taken]
+                    assert n <= s + 1
+                    sum_unit(n, h)
+                    if h == 1:
+                        done.append(n)
+                    taken += 1
+            if s > 0:
+                scale_bank(s, 0)
+                scale_bank(s, 1)
+            if s + 2 < TILES:
+                transposes(s + 2)
+                if s + 2 not in NATURAL:
+                    squares(s + 2, 0)
+                    squares(s + 2, 1)
+            for n in done:
+                reduce_sum(n)
+            if s >= 1:
+                quantise(s - 1)
+            if s >= 2:
+                stage1(s - 1)
+            if s < 2:
+                spread_rls(2 * s)
+                spread_rls(2 * s + 1)
+            if s == 15:
+                for c in range(2):
+                    acc = ps_t.tile([P, 512], F32, tag="t", name="acc")
+                    accs.append(acc)
+                    stage2(0, c)
+                    stage2(1, c)
+            run(s, "mid")
+        assert taken == len(units)
+
+        quantise(16)
+        stage1(16)
+        stage2(2, 0)
+        stage2(2, 1)
+        for c in range(2, 4):
+            acc = ps_t.tile([P, 512], F32, tag="t", name="acc")
+            accs.append(acc)
             for g in range(3):
                 stage2(g, c)
         add_xsq(3)

@@ -17,7 +17,10 @@ D = 2048
 NK = 2048
 TILES = 17
 FLOPS = 2 * 128 * 2048 * 2048 * 2
-NATURAL = (4, 8, 12, 16)
+NATURAL = (7, 11, 14, 16)
+PLANES = ()
+FIRST_CHUNK_STEP = 4
+CHUNK_STEPS = 10
 
 
 def tile_gpytorchrbfkernelffn_w_kernel(tc, x, centers, lengthscale, W_out_words, W_out_scales, b_out, out):
@@ -73,11 +76,15 @@ def tile_gpytorchrbfkernelffn_w_kernel(tc, x, centers, lengthscale, W_out_words,
         junk = keep.tile([P, P], F32)
         junk2 = keep.tile([P, D], BF16)
         rls_b = keep.tile([P, D], F32)
-        wide = {}
         x_codes = keep.tile([P, 512], U32, align_bytes=64)
         x_plane = keep.tile([P, 512], U8, align_bytes=64)
-        k_codes = keep.tile([P, 4, P], U32, align_bytes=64)
-        k_plane = keep.tile([P, 4, P], U8, align_bytes=64)
+        k_codes = []
+        k_plane = []
+        for g in range(4):
+            kc = keep.tile([P, P], U32, name="k_codes%d" % g, align_bytes=64)
+            kp = keep.tile([P, P], U8, name="k_plane%d" % g, align_bytes=64)
+            k_codes.append(kc)
+            k_plane.append(kp)
 
         tab_t = ps_r.tile([P, 512], F32, tag="r")
         nc.tensor.transpose(tab_t[:, 0:P], tab[:].bitcast(F32), ident[:])
@@ -86,13 +93,16 @@ def tile_gpytorchrbfkernelffn_w_kernel(tc, x, centers, lengthscale, W_out_words,
 
         banks = {}
         squared = {}
+        scaled = {}
         sums = {}
+        wide = {}
         grouped = {}
         codes = {}
         z_bank = {}
         z1s = {}
         exps = {}
         kgs = {}
+        have = set()
 
         def transposes(n):
             words = nat[n][:].bitcast(F32)
@@ -104,14 +114,17 @@ def tile_gpytorchrbfkernelffn_w_kernel(tc, x, centers, lengthscale, W_out_words,
                         nc.tensor.transpose(tb[:, u, gg, :], words[:, P * w : P * w + P], ident[:])
                 banks[(n, h)] = tb
 
-        def squares(n, h):
-            sq = ring.tile([P, 8, P], F32, tag="sq", name="sq", bufs=6)
-            view = (
+        def by_plane(n, h):
+            return (
                 banks[(n, h)][:]
                 .rearrange("p u g j -> p (u g j)")
                 .bitcast(BF16)
                 .rearrange("p (u g j e) -> p u g e j", u=2, g=2, j=P, e=2)
             )
+
+        def squares(n, h):
+            sq = ring.tile([P, 8, P], F32, tag="sq", name="sq", bufs=6)
+            view = by_plane(n, h)
             for u in range(2):
                 for gg in range(2):
                     for e in range(2):
@@ -123,6 +136,21 @@ def tile_gpytorchrbfkernelffn_w_kernel(tc, x, centers, lengthscale, W_out_words,
                             scale=rls_t[:, c : c + 1],
                         )
             squared[(n, h)] = sq
+
+        def scale_planes(n, h):
+            sp = ring.tile([P, 2, 4, P], BF16, tag="sp", name="sp", bufs=4)
+            view = by_plane(n, h)
+            for u in range(2):
+                for gg in range(2):
+                    for e in range(2):
+                        c = 4 * (2 * h + gg) + 2 * u + e
+                        nc.scalar.activation(
+                            out=sp[:, gg, 2 * u + e, :],
+                            in_=view[:, u, gg, e, :],
+                            func=ACT.Copy,
+                            scale=rls_t[:, c : c + 1],
+                        )
+            scaled[(n, h)] = sp
 
         def sum_unit(n, h):
             if h == 0:
@@ -136,6 +164,10 @@ def tile_gpytorchrbfkernelffn_w_kernel(tc, x, centers, lengthscale, W_out_words,
                     start=(h == 0 and k == 0),
                     stop=(h == 1 and k == 7),
                 )
+
+        def reduce_sum(n):
+            nc.scalar.activation(out=junk[:], in_=sums[n][:, 0:P], func=ACT.Copy, accum_out=csq[:, n : n + 1])
+            have.add(n)
 
         def spread_rls(b):
             pb = ps_z.tile([P, 4, P], F32, tag="z", name="pb")
@@ -155,13 +187,17 @@ def tile_gpytorchrbfkernelffn_w_kernel(tc, x, centers, lengthscale, W_out_words,
 
         def square_sum(n):
             nc.scalar.activation(out=junk2[:], in_=wide[n][:], func=ACT.Square, accum_out=csq[:, n : n + 1])
-
-        def reduce_sum(n):
-            nc.scalar.activation(out=junk[:], in_=sums[n][:, 0:P], func=ACT.Copy, accum_out=csq[:, n : n + 1])
+            have.add(n)
 
         def scale_bank(n, h):
             if n not in grouped:
                 grouped[n] = ring.tile([P, 4, P, 4], BF16, tag="grouped", name="gr", align_bytes=64)
+            if n in PLANES:
+                nc.vector.tensor_copy(
+                    out=grouped[n][:, 2 * h : 2 * h + 2, :, :].rearrange("p g (c i) t -> p g c t i", i=4),
+                    in_=scaled[(n, h)][:].rearrange("p g t (c i) -> p g c t i", i=4),
+                )
+                return
             nc.vector.tensor_tensor(
                 out=grouped[n][:, 2 * h : 2 * h + 2, :, :].rearrange("p g j (u e) -> p g j u e", u=2, e=2),
                 in0=banks[(n, h)][:]
@@ -204,40 +240,45 @@ def tile_gpytorchrbfkernelffn_w_kernel(tc, x, centers, lengthscale, W_out_words,
                 )
 
         def halve(lo, hi):
+            for n in range(lo, hi):
+                assert n in have
             nc.scalar.mul(out=nh[:, lo:hi], in_=csq[:, lo:hi], mul=-0.5)
 
-        def add_xsq(g):
-            z1 = work.tile([P, 4, P], F32, tag="z1", name="z1")
+        def exponent(arg):
+            g, t0, t1 = arg
+            if t0 == 0:
+                z1s[g] = work.tile([P, 4, P], F32, tag="z1", name="z1")
+                exps[g] = work.tile([P, 4, P], F32, tag="ex", name="ex")
             nc.vector.tensor_tensor(
-                out=z1[:], in0=z_bank[g][:], in1=nhx_b[:].unsqueeze(1).to_broadcast([P, 4, P]), op=ALU.add
+                out=z1s[g][:, t0:t1, :],
+                in0=z_bank[g][:, t0:t1, :],
+                in1=nhx_b[:].unsqueeze(1).to_broadcast([P, t1 - t0, P]),
+                op=ALU.add,
             )
-            z1s[g] = z1
-
-        def exponentials(g):
-            halve(4 * g + 1, 4 * g + 5)
-            ex = work.tile([P, 4, P], F32, tag="ex", name="ex")
-            for t in range(4):
+            halve(4 * g + 1 + t0, 4 * g + 1 + t1)
+            for t in range(t0, t1):
                 n = 4 * g + t + 1
                 nc.scalar.activation(
-                    out=ex[:, t, :], in_=z1s[g][:, t, :], func=ACT.Exp, bias=nh[:, n : n + 1], scale=1.0
+                    out=exps[g][:, t, :], in_=z1s[g][:, t, :], func=ACT.Exp, bias=nh[:, n : n + 1], scale=1.0
                 )
-            exps[g] = ex
 
         def clamp(g):
             kg = work.tile([P, P, 4], BF16, tag="kg", name="kg", align_bytes=64)
-            nc.vector.tensor_scalar(
-                out=kg[:], in0=exps[g][:].rearrange("p t i -> p i t"), scalar1=1.0, scalar2=None, op0=ALU.min
-            )
+            view = exps[g][:].rearrange("p t i -> p i t")
+            if g < 3:
+                nc.gpsimd.tensor_scalar(out=kg[:], in0=view, scalar1=1.0, scalar2=0.0, op0=ALU.min, op1=ALU.max)
+            else:
+                nc.vector.tensor_scalar(out=kg[:], in0=view, scalar1=1.0, scalar2=None, op0=ALU.min)
             kgs[g] = kg
 
         def quantise_k(g):
             nc.vector.quantize_mx(
-                out=k_codes[:, g, :].bitcast(FP8X4), scales=k_plane[:, g, :], in_=kgs[g][:].rearrange("p i t -> p (i t)")
+                out=k_codes[g][:].bitcast(FP8X4), scales=k_plane[g][:], in_=kgs[g][:].rearrange("p i t -> p (i t)")
             )
 
         def spread_xsq(unused):
             halve(0, 1)
-            pm = ps_z.tile([P, 512], F32, tag="z", name="pm")
+            pm = ps_r.tile([P, 512], F32, tag="r", name="pm")
             nc.tensor.transpose(pm[:, 0:P], nh[:, 0:1].to_broadcast([P, P]), ident[:])
             banks["xsq"] = pm
 
@@ -256,30 +297,28 @@ def tile_gpytorchrbfkernelffn_w_kernel(tc, x, centers, lengthscale, W_out_words,
             for fn, arg in events.get((step, where), []):
                 fn(arg)
 
-        at(1, "mid", spread_xsq, 0)
-        at(5, "early", copy_xsq, 0)
+        at(2, "mid", spread_xsq, 0)
+        at(4, "early", copy_xsq, 0)
         for g in range(3):
-            at(4 * g + 6, "mid", add_xsq, g)
-            at(4 * g + 6, "mid", exponentials, g)
-            at(4 * g + 7, "early", clamp, g)
-            at(4 * g + 7, "mid", quantise_k, g)
-        for n in NATURAL:
+            at(4 * g + 6, "mid", exponent, (g, 0, 4))
+            at(4 * g + 6, "mid", clamp, g)
+            at(4 * g + 8, "mid", quantise_k, g)
+        at(16, "early", exponent, (3, 0, 2))
+        for k, n in enumerate(NATURAL):
             for c in range(4):
-                at(n - 3 + c, "early", natural_chunk, (n, c))
-            if n < 16:
-                at(n + 1, "early", square_sum, n)
-            else:
-                at(n, "mid", square_sum, n)
+                step = FIRST_CHUNK_STEP + (CHUNK_STEPS * (4 * k + c)) // (4 * len(NATURAL))
+                at(step, "early", natural_chunk, (n, c))
+            at(step, "mid", square_sum, n)
 
-        units = [(n, h) for n in range(1, TILES) if n not in NATURAL for h in range(2)]
+        units = []
         taken = 0
         accs = []
 
         def stage2(g, c):
             nc.tensor.matmul_mx(
                 out=accs[c][:],
-                lhsT=k_codes[:, g, :].bitcast(FP8X4),
-                lhsT_scale=k_plane[:, g, :],
+                lhsT=k_codes[g][:].bitcast(FP8X4),
+                lhsT_scale=k_plane[g][:],
                 rhs=w_words[g][:, 2048 * c : 2048 * c + 2048].bitcast(FP8X4),
                 rhs_scale=planes[4 * g : P, 512 * c : 512 * c + 512],
                 start=(g == 0),
@@ -288,34 +327,29 @@ def tile_gpytorchrbfkernelffn_w_kernel(tc, x, centers, lengthscale, W_out_words,
 
         transposes(0)
         transposes(1)
-        squares(0, 0)
-        scale_bank(0, 1)
-        scale_bank(0, 0)
-        squares(0, 1)
-        sum_unit(0, 0)
-        sum_unit(0, 1)
-        squares(1, 0)
-        squares(1, 1)
-        reduce_sum(0)
         for s in range(TILES):
             run(s, "early")
             done = []
-            for k in range(2 - s % 2):
+            for k in range(2):
                 if taken < len(units):
                     n, h = units[taken]
-                    assert n <= s + 1
                     sum_unit(n, h)
                     if h == 1:
                         done.append(n)
                     taken += 1
-            if s > 0:
-                scale_bank(s, 0)
-                scale_bank(s, 1)
+            for h in range(2):
+                scale_bank(s, h)
+                if s not in NATURAL and s not in PLANES:
+                    squares(s, h)
+                    units.append((s, h))
+            if s + 1 in PLANES:
+                for h in range(2):
+                    scale_planes(s + 1, h)
+                    if s + 1 not in NATURAL:
+                        squares(s + 1, h)
+                        units.append((s + 1, h))
             if s + 2 < TILES:
                 transposes(s + 2)
-                if s + 2 not in NATURAL:
-                    squares(s + 2, 0)
-                    squares(s + 2, 1)
             for n in done:
                 reduce_sum(n)
             if s >= 1:
@@ -343,8 +377,7 @@ def tile_gpytorchrbfkernelffn_w_kernel(tc, x, centers, lengthscale, W_out_words,
             accs.append(acc)
             for g in range(3):
                 stage2(g, c)
-        add_xsq(3)
-        exponentials(3)
+        exponent((3, 2, 4))
         clamp(3)
         quantise_k(3)
         out_rows = out.rearrange("b l n -> (b l) n")

@@ -17,10 +17,7 @@ D = 2048
 NK = 2048
 TILES = 17
 FLOPS = 2 * 128 * 2048 * 2048 * 2
-NATURAL = (7, 11, 14, 16)
-PLANES = ()
-FIRST_CHUNK_STEP = 4
-CHUNK_STEPS = 10
+NAT0 = 1536
 
 
 def tile_gpytorchrbfkernelffn_w_kernel(tc, x, centers, lengthscale, W_out_words, W_out_scales, b_out, out):
@@ -29,7 +26,7 @@ def tile_gpytorchrbfkernelffn_w_kernel(tc, x, centers, lengthscale, W_out_words,
         ctx.enter_context(tc.manual_schedule())
         keep = ctx.enter_context(tc.tile_pool(name="keep", bufs=1))
         work = ctx.enter_context(tc.tile_pool(name="work", bufs=2))
-        ring = ctx.enter_context(tc.tile_pool(name="ring", bufs=3))
+        ring = ctx.enter_context(tc.tile_pool(name="ring", bufs=4))
         ps_t = ctx.enter_context(tc.psum_pool(name="ps_t", bufs=4))
         ps_z = ctx.enter_context(tc.psum_pool(name="ps_z", bufs=2))
         ps_r = ctx.enter_context(tc.psum_pool(name="ps_r", bufs=2))
@@ -70,12 +67,14 @@ def tile_gpytorchrbfkernelffn_w_kernel(tc, x, centers, lengthscale, W_out_words,
 
         ls_t = keep.tile([P, 16], F32)
         rls_t = keep.tile([P, 16], F32)
-        csq = keep.tile([P, TILES], F32)
+        rls_n = keep.tile([P, D - NAT0], F32)
+        csq_t = keep.tile([P, TILES], F32)
+        csq_n = keep.tile([P, TILES], F32)
+        nh_n = keep.tile([P, TILES], F32)
         nh = keep.tile([P, TILES], F32)
         nhx_b = keep.tile([P, P], F32)
         junk = keep.tile([P, P], F32)
-        junk2 = keep.tile([P, D], BF16)
-        rls_b = keep.tile([P, D], F32)
+        junk2 = keep.tile([P, D - NAT0], BF16)
         x_codes = keep.tile([P, 512], U32, align_bytes=64)
         x_plane = keep.tile([P, 512], U8, align_bytes=64)
         k_codes = []
@@ -93,16 +92,13 @@ def tile_gpytorchrbfkernelffn_w_kernel(tc, x, centers, lengthscale, W_out_words,
 
         banks = {}
         squared = {}
-        scaled = {}
         sums = {}
-        wide = {}
         grouped = {}
         codes = {}
         z_bank = {}
         z1s = {}
         exps = {}
         kgs = {}
-        have = set()
 
         def transposes(n):
             words = nat[n][:].bitcast(F32)
@@ -114,90 +110,63 @@ def tile_gpytorchrbfkernelffn_w_kernel(tc, x, centers, lengthscale, W_out_words,
                         nc.tensor.transpose(tb[:, u, gg, :], words[:, P * w : P * w + P], ident[:])
                 banks[(n, h)] = tb
 
-        def by_plane(n, h):
-            return (
+        def spread_rls():
+            pb = ps_z.tile([P, 4, P], F32, tag="z", name="pb")
+            for k in range(4):
+                nc.tensor.transpose(pb[:, k, :], rls_t[:, 12 + k : 13 + k].to_broadcast([P, P]), ident[:])
+            nc.scalar.copy(
+                out=rls_n[:].rearrange("p (u q e) -> p u q e", u=2, q=P, e=2),
+                in_=pb[:].rearrange("p (u e) q -> p u q e", u=2, e=2),
+            )
+
+        def natural_part(n):
+            wv = ring.tile([P, D - NAT0], F32, tag="wv", name="wv")
+            nc.vector.tensor_tensor(out=wv[:], in0=nat[n][:, NAT0:D], in1=rls_n[:], op=ALU.mult)
+            nc.scalar.activation(out=junk2[:], in_=wv[:], func=ACT.Square, accum_out=csq_n[:, n : n + 1])
+            nc.scalar.mul(out=nh_n[:, n : n + 1], in_=csq_n[:, n : n + 1], mul=-0.5)
+
+        def squares(n, h):
+            sq = ring.tile([P, 8, P], F32, tag="sq", name="sq")
+            view = (
                 banks[(n, h)][:]
                 .rearrange("p u g j -> p (u g j)")
                 .bitcast(BF16)
                 .rearrange("p (u g j e) -> p u g e j", u=2, g=2, j=P, e=2)
             )
-
-        def squares(n, h):
-            sq = ring.tile([P, 8, P], F32, tag="sq", name="sq", bufs=6)
-            view = by_plane(n, h)
-            for u in range(2):
-                for gg in range(2):
+            k = 0
+            for gg in range(2 - h):
+                for u in range(2):
                     for e in range(2):
                         c = 4 * (2 * h + gg) + 2 * u + e
                         nc.scalar.activation(
-                            out=sq[:, 4 * u + 2 * gg + e, :],
-                            in_=view[:, u, gg, e, :],
-                            func=ACT.Square,
-                            scale=rls_t[:, c : c + 1],
+                            out=sq[:, k, :], in_=view[:, u, gg, e, :], func=ACT.Square, scale=rls_t[:, c : c + 1]
                         )
+                        k += 1
             squared[(n, h)] = sq
 
-        def scale_planes(n, h):
-            sp = ring.tile([P, 2, 4, P], BF16, tag="sp", name="sp", bufs=4)
-            view = by_plane(n, h)
-            for u in range(2):
-                for gg in range(2):
-                    for e in range(2):
-                        c = 4 * (2 * h + gg) + 2 * u + e
-                        nc.scalar.activation(
-                            out=sp[:, gg, 2 * u + e, :],
-                            in_=view[:, u, gg, e, :],
-                            func=ACT.Copy,
-                            scale=rls_t[:, c : c + 1],
-                        )
-            scaled[(n, h)] = sp
+        def sum_planes(n):
+            rt = ps_r.tile([P, 512], F32, tag="r", name="rt")
+            for h in range(2):
+                for k in range(8 - 4 * h):
+                    nc.tensor.matmul(
+                        out=rt[:, 0:P],
+                        lhsT=squared[(n, h)][:, k, :],
+                        rhs=ident[:],
+                        is_transpose=True,
+                        start=(h == 0 and k == 0),
+                        stop=(h == 1 and k == 3),
+                    )
+            sums[n] = rt
 
-        def sum_unit(n, h):
-            if h == 0:
-                sums[n] = ps_r.tile([P, 512], F32, tag="r", name="rt")
-            for k in range(8):
-                nc.tensor.matmul(
-                    out=sums[n][:, 0:P],
-                    lhsT=squared[(n, h)][:, k, :],
-                    rhs=ident[:],
-                    is_transpose=True,
-                    start=(h == 0 and k == 0),
-                    stop=(h == 1 and k == 7),
-                )
-
-        def reduce_sum(n):
-            nc.scalar.activation(out=junk[:], in_=sums[n][:, 0:P], func=ACT.Copy, accum_out=csq[:, n : n + 1])
-            have.add(n)
-
-        def spread_rls(b):
-            pb = ps_z.tile([P, 4, P], F32, tag="z", name="pb")
-            for k in range(4):
-                nc.tensor.transpose(pb[:, k, :], rls_t[:, 4 * b + k : 4 * b + k + 1].to_broadcast([P, P]), ident[:])
-            nc.scalar.copy(
-                out=rls_b[:, 512 * b : 512 * b + 512].rearrange("p (u q e) -> p u q e", u=2, q=P, e=2),
-                in_=pb[:].rearrange("p (u e) q -> p u q e", u=2, e=2),
+        def finish_sum(n):
+            nc.scalar.activation(out=junk[:], in_=sums[n][:, 0:P], func=ACT.Copy, accum_out=csq_t[:, n : n + 1])
+            nc.scalar.activation(
+                out=nh[:, n : n + 1], in_=csq_t[:, n : n + 1], func=ACT.Identity, scale=-0.5, bias=nh_n[:, n : n + 1]
             )
 
-        def natural_chunk(arg):
-            n, c = arg
-            if c == 0:
-                wide[n] = work.tile([P, D], F32, tag="wv", name="wv")
-            cols = slice(512 * c, 512 * c + 512)
-            nc.vector.tensor_tensor(out=wide[n][:, cols], in0=nat[n][:, cols], in1=rls_b[:, cols], op=ALU.mult)
-
-        def square_sum(n):
-            nc.scalar.activation(out=junk2[:], in_=wide[n][:], func=ACT.Square, accum_out=csq[:, n : n + 1])
-            have.add(n)
-
         def scale_bank(n, h):
-            if n not in grouped:
+            if h == 0:
                 grouped[n] = ring.tile([P, 4, P, 4], BF16, tag="grouped", name="gr", align_bytes=64)
-            if n in PLANES:
-                nc.vector.tensor_copy(
-                    out=grouped[n][:, 2 * h : 2 * h + 2, :, :].rearrange("p g (c i) t -> p g c t i", i=4),
-                    in_=scaled[(n, h)][:].rearrange("p g t (c i) -> p g c t i", i=4),
-                )
-                return
             nc.vector.tensor_tensor(
                 out=grouped[n][:, 2 * h : 2 * h + 2, :, :].rearrange("p g j (u e) -> p g j u e", u=2, e=2),
                 in0=banks[(n, h)][:]
@@ -239,13 +208,7 @@ def tile_gpytorchrbfkernelffn_w_kernel(tc, x, centers, lengthscale, W_out_words,
                     stop=(c == 3),
                 )
 
-        def halve(lo, hi):
-            for n in range(lo, hi):
-                assert n in have
-            nc.scalar.mul(out=nh[:, lo:hi], in_=csq[:, lo:hi], mul=-0.5)
-
-        def exponent(arg):
-            g, t0, t1 = arg
+        def exponent(g, t0, t1):
             if t0 == 0:
                 z1s[g] = work.tile([P, 4, P], F32, tag="z1", name="z1")
                 exps[g] = work.tile([P, 4, P], F32, tag="ex", name="ex")
@@ -255,7 +218,6 @@ def tile_gpytorchrbfkernelffn_w_kernel(tc, x, centers, lengthscale, W_out_words,
                 in1=nhx_b[:].unsqueeze(1).to_broadcast([P, t1 - t0, P]),
                 op=ALU.add,
             )
-            halve(4 * g + 1 + t0, 4 * g + 1 + t1)
             for t in range(t0, t1):
                 n = 4 * g + t + 1
                 nc.scalar.activation(
@@ -276,42 +238,6 @@ def tile_gpytorchrbfkernelffn_w_kernel(tc, x, centers, lengthscale, W_out_words,
                 out=k_codes[g][:].bitcast(FP8X4), scales=k_plane[g][:], in_=kgs[g][:].rearrange("p i t -> p (i t)")
             )
 
-        def spread_xsq(unused):
-            halve(0, 1)
-            pm = ps_r.tile([P, 512], F32, tag="r", name="pm")
-            nc.tensor.transpose(pm[:, 0:P], nh[:, 0:1].to_broadcast([P, P]), ident[:])
-            banks["xsq"] = pm
-
-        def copy_xsq(unused):
-            nc.vector.tensor_copy(out=nhx_b[:], in_=banks["xsq"][:, 0:P])
-
-        events = {}
-
-        def at(step, where, fn, arg):
-            key = (step, where)
-            if key not in events:
-                events[key] = []
-            events[key].append((fn, arg))
-
-        def run(step, where):
-            for fn, arg in events.get((step, where), []):
-                fn(arg)
-
-        at(2, "mid", spread_xsq, 0)
-        at(4, "early", copy_xsq, 0)
-        for g in range(3):
-            at(4 * g + 6, "mid", exponent, (g, 0, 4))
-            at(4 * g + 6, "mid", clamp, g)
-            at(4 * g + 8, "mid", quantise_k, g)
-        at(16, "early", exponent, (3, 0, 2))
-        for k, n in enumerate(NATURAL):
-            for c in range(4):
-                step = FIRST_CHUNK_STEP + (CHUNK_STEPS * (4 * k + c)) // (4 * len(NATURAL))
-                at(step, "early", natural_chunk, (n, c))
-            at(step, "mid", square_sum, n)
-
-        units = []
-        taken = 0
         accs = []
 
         def stage2(g, c):
@@ -326,47 +252,53 @@ def tile_gpytorchrbfkernelffn_w_kernel(tc, x, centers, lengthscale, W_out_words,
             )
 
         transposes(0)
-        transposes(1)
+        spread_rls()
         for s in range(TILES):
-            run(s, "early")
-            done = []
-            for k in range(2):
-                if taken < len(units):
-                    n, h = units[taken]
-                    sum_unit(n, h)
-                    if h == 1:
-                        done.append(n)
-                    taken += 1
-            for h in range(2):
-                scale_bank(s, h)
-                if s not in NATURAL and s not in PLANES:
-                    squares(s, h)
-                    units.append((s, h))
-            if s + 1 in PLANES:
-                for h in range(2):
-                    scale_planes(s + 1, h)
-                    if s + 1 not in NATURAL:
-                        squares(s + 1, h)
-                        units.append((s + 1, h))
-            if s + 2 < TILES:
-                transposes(s + 2)
-            for n in done:
-                reduce_sum(n)
+            if s == 3:
+                nc.vector.tensor_copy(out=nhx_b[:], in_=banks["xsq"][:, 0:P])
+            if s >= 1:
+                sum_planes(s - 1)
+            if s == 16:
+                sum_planes(16)
+            if s + 1 < TILES:
+                transposes(s + 1)
+            scale_bank(s, 0)
+            if s < 16:
+                squares(s, 0)
+            if s >= 1:
+                finish_sum(s - 1)
+            scale_bank(s, 1)
+            if s < 16:
+                squares(s, 1)
+            natural_part(s)
+            if s == 15:
+                squares(16, 0)
+                squares(16, 1)
+            if s == 16:
+                finish_sum(16)
+                exponent(3, 0, 2)
             if s >= 1:
                 quantise(s - 1)
-            if s >= 2:
+            if s >= 3 and s % 2 == 1:
+                stage1(s - 2)
                 stage1(s - 1)
-            if s < 2:
-                spread_rls(2 * s)
-                spread_rls(2 * s + 1)
+            if s == 16:
+                stage1(15)
+            if s == 1:
+                pm = ps_r.tile([P, 512], F32, tag="r", name="pm")
+                nc.tensor.transpose(pm[:, 0:P], nh[:, 0:1].to_broadcast([P, P]), ident[:])
+                banks["xsq"] = pm
             if s == 15:
                 for c in range(2):
                     acc = ps_t.tile([P, 512], F32, tag="t", name="acc")
                     accs.append(acc)
                     stage2(0, c)
                     stage2(1, c)
-            run(s, "mid")
-        assert taken == len(units)
+            if s >= 6 and s % 4 == 2 and s < 16:
+                exponent((s - 6) // 4, 0, 4)
+                clamp((s - 6) // 4)
+            if s >= 8 and s % 4 == 0:
+                quantise_k((s - 8) // 4)
 
         quantise(16)
         stage1(16)
@@ -377,7 +309,7 @@ def tile_gpytorchrbfkernelffn_w_kernel(tc, x, centers, lengthscale, W_out_words,
             accs.append(acc)
             for g in range(3):
                 stage2(g, c)
-        exponent((3, 2, 4))
+        exponent(3, 2, 4)
         clamp(3)
         quantise_k(3)
         out_rows = out.rearrange("b l n -> (b l) n")

@@ -184,8 +184,8 @@ def tile_gpytorchrbfkernelffn_w_kernel(tc, x, centers, lengthscale, W_out_words,
             if n == 0:
                 cd, pl = x_codes, x_plane
             else:
-                cd = ring.tile([P, 512], U32, tag="codes", name="cd", align_bytes=64)
-                pl = ring.tile([P, 512], U8, tag="plane", name="pl", align_bytes=64)
+                cd = ring.tile([P, 512], U32, tag="codes", name="cd", align_bytes=64, bufs=6)
+                pl = ring.tile([P, 512], U8, tag="plane", name="pl", align_bytes=64, bufs=6)
             codes[n] = (cd, pl)
             nc.vector.quantize_mx(
                 out=cd[:].bitcast(FP8X4), scales=pl[:], in_=grouped[n][:].rearrange("p g j t -> p (g j t)")
@@ -227,10 +227,7 @@ def tile_gpytorchrbfkernelffn_w_kernel(tc, x, centers, lengthscale, W_out_words,
         def clamp(g):
             kg = work.tile([P, P, 4], BF16, tag="kg", name="kg", align_bytes=64)
             view = exps[g][:].rearrange("p t i -> p i t")
-            if g < 3:
-                nc.gpsimd.tensor_scalar(out=kg[:], in0=view, scalar1=1.0, scalar2=0.0, op0=ALU.min, op1=ALU.max)
-            else:
-                nc.vector.tensor_scalar(out=kg[:], in0=view, scalar1=1.0, scalar2=None, op0=ALU.min)
+            nc.vector.tensor_scalar(out=kg[:], in0=view, scalar1=1.0, scalar2=None, op0=ALU.min)
             kgs[g] = kg
 
         def quantise_k(g):
@@ -279,9 +276,12 @@ def tile_gpytorchrbfkernelffn_w_kernel(tc, x, centers, lengthscale, W_out_words,
                 exponent(3, 0, 2)
             if s >= 1:
                 quantise(s - 1)
-            if s >= 3 and s % 2 == 1:
-                stage1(s - 2)
-                stage1(s - 1)
+            if s >= 5 and s % 4 == 1 and s < 15:
+                for n in range(s - 4, s):
+                    stage1(n)
+            if s == 15:
+                stage1(13)
+                stage1(14)
             if s == 16:
                 stage1(15)
             if s == 1:
@@ -296,7 +296,8 @@ def tile_gpytorchrbfkernelffn_w_kernel(tc, x, centers, lengthscale, W_out_words,
                     stage2(1, c)
             if s >= 6 and s % 4 == 2 and s < 16:
                 exponent((s - 6) // 4, 0, 4)
-                clamp((s - 6) // 4)
+            if s >= 7 and s % 4 == 3:
+                clamp((s - 7) // 4)
             if s >= 8 and s % 4 == 0:
                 quantise_k((s - 8) // 4)
 

@@ -33,6 +33,7 @@ def tile_gpytorchrbfkernelffn_w_kernel(tc, x, centers, lengthscale, W_out_words,
 
         tab = keep.tile([P, 256], BF16)
         nc.vector.memset(tab[:], 0.0)
+        nc.scalar.dma_start(out=tab[0:8, :], in_=lengthscale.rearrange("(w q) -> w q", q=256))
         planes = keep.tile([P, NK], U8, align_bytes=64)
         nc.vector.memset(planes[:].bitcast(I32), 0)
         warm = keep.tile([P, 1], F32)
@@ -42,10 +43,11 @@ def tile_gpytorchrbfkernelffn_w_kernel(tc, x, centers, lengthscale, W_out_words,
         ident = keep.tile([P, P], F32)
         make_identity(nc, ident[:])
 
-        nc.sync.dma_start(out=tab[0:8, :], in_=lengthscale.rearrange("(w q) -> w q", q=256))
         nat = []
         x_nat = keep.tile([P, D], BF16)
-        nc.sync.dma_start(out=x_nat[:], in_=x.rearrange("b l d -> (b l) d"))
+        x_rows = x.rearrange("b l d -> (b l) d")
+        nc.sync.dma_start(out=x_nat[:, 0:1024], in_=x_rows[:, 0:1024])
+        nc.sync.dma_start(out=x_nat[:, 1024:D], in_=x_rows[:, 1024:D])
         nat.append(x_nat)
         c_view = centers.rearrange("(g p t) d -> g p t d", p=P, t=4)
         for n in range(1, TILES):

from contextlib import ExitStack

import concourse.mybir as mybir
from concourse.masks import make_identity

F32 = mybir.dt.float32
BF16 = mybir.dt.bfloat16
U8 = mybir.dt.uint8
U32 = mybir.dt.uint32
I32 = mybir.dt.int32
FP8X4 = mybir.dt.float8_e4m3fn_x4
ACT = mybir.ActivationFunctionType
ALU = mybir.AluOpType

P = 128
D = 2048
NK = 2048
TILES = 17
FLOPS = 2 * 128 * 2048 * 2048 * 2
NAT0 = 1536


def tile_gpytorchrbfkernelffn_w_kernel(tc, x, centers, lengthscale, W_out_words, W_out_scales, b_out, out):
    nc = tc.nc
    with ExitStack() as ctx:
        ctx.enter_context(tc.manual_schedule())
        keep = ctx.enter_context(tc.tile_pool(name="keep", bufs=1))
        work = ctx.enter_context(tc.tile_pool(name="work", bufs=2))
        ring = ctx.enter_context(tc.tile_pool(name="ring", bufs=4))
        ps_t = ctx.enter_context(tc.psum_pool(name="ps_t", bufs=4))
        ps_z = ctx.enter_context(tc.psum_pool(name="ps_z", bufs=2))
        ps_r = ctx.enter_context(tc.psum_pool(name="ps_r", bufs=2))

        tab = keep.tile([P, 256], BF16)
        nc.vector.memset(tab[:], 0.0)
        nc.scalar.dma_start(out=tab[0:8, :], in_=lengthscale.rearrange("(w q) -> w q", q=256))
        planes = keep.tile([P, NK], U8, align_bytes=64)
        nc.vector.memset(planes[:].bitcast(I32), 0)
        warm = keep.tile([P, 1], F32)
        nc.vector.memset(warm[:], 0.0)
        warm2 = keep.tile([P, 1], F32)
        nc.scalar.activation(out=warm2[:], in_=warm[:], func=ACT.Exp)
        ident = keep.tile([P, P], F32)
        make_identity(nc, ident[:])

        nat = []
        x_nat = keep.tile([P, D], BF16)
        x_rows = x.rearrange("b l d -> (b l) d")
        nc.sync.dma_start(out=x_nat[:, 0:1024], in_=x_rows[:, 0:1024])
        nc.sync.dma_start(out=x_nat[:, 1024:D], in_=x_rows[:, 1024:D])
        nat.append(x_nat)
        c_view = centers.rearrange("(g p t) d -> g p t d", p=P, t=4)
        for n in range(1, TILES):
            c_nat = keep.tile([P, D], BF16, name="c_nat%d" % n)
            nc.sync.dma_start(out=c_nat[:], in_=c_view[(n - 1) // 4, :, (n - 1) % 4, :])
            nat.append(c_nat)
        for q in range(4):
            nc.sync.dma_start(
                out=planes[32 * q : 32 * q + 16, :].bitcast(I32),
                in_=W_out_scales[:, 4 * q : 4 * q + 4, :].bitcast(I32),
            )
        w_words = []
        for g in range(4):
            ww = keep.tile([P, 4 * NK], U8, name="w_words%d" % g, align_bytes=64)
            nc.sync.dma_start(out=ww[:].bitcast(I32), in_=W_out_words[g].rearrange("p n t -> p (n t)").bitcast(I32))
            w_words.append(ww)
        bias_b = keep.tile([P, NK], BF16)
        nc.sync.dma_start(out=bias_b[:], in_=b_out.partition_broadcast(P))

        ls_t = keep.tile([P, 16], F32)
        rls_t = keep.tile([P, 16], F32)
        rls_n = keep.tile([P, D - NAT0], F32)
        csq_t = keep.tile([P, TILES], F32)
        csq_n = keep.tile([P, TILES], F32)
        nh_n = keep.tile([P, TILES], F32)
        nh = keep.tile([P, TILES], F32)
        nhx_b = keep.tile([P, P], F32)
        junk = keep.tile([P, P], F32)
        junk2 = keep.tile([P, D - NAT0], BF16)
        x_codes = keep.tile([P, 512], U32, align_bytes=64)
        x_plane = keep.tile([P, 512], U8, align_bytes=64)
        k_codes = []
        k_plane = []
        for g in range(4):
            kc = keep.tile([P, P], U32, name="k_codes%d" % g, align_bytes=64)
            kp = keep.tile([P, P], U8, name="k_plane%d" % g, align_bytes=64)
            k_codes.append(kc)
            k_plane.append(kp)

        tab_t = ps_r.tile([P, 512], F32, tag="r")
        nc.tensor.transpose(tab_t[:, 0:P], tab[:].bitcast(F32), ident[:])
        nc.vector.tensor_copy(out=ls_t[:], in_=tab_t[:, 0:8].bitcast(BF16))
        nc.vector.reciprocal(out=rls_t[:], in_=ls_t[:])

        banks = {}
        squared = {}
        sums = {}
        grouped = {}
        codes = {}
        z_bank = {}
        z1s = {}
        exps = {}
        kgs = {}

        def transposes(n):
            words = nat[n][:].bitcast(F32)
            for h in range(2):
                tb = ps_t.tile([P, 2, 2, P], F32, tag="t", name="tb")
                for u in range(2):
                    for gg in range(2):
                        w = 2 * (2 * h + gg) + u
                        nc.tensor.transpose(tb[:, u, gg, :], words[:, P * w : P * w + P], ident[:])
                banks[(n, h)] = tb

        def spread_rls():
            pb = ps_z.tile([P, 4, P], F32, tag="z", name="pb")
            for k in range(4):
                nc.tensor.transpose(pb[:, k, :], rls_t[:, 12 + k : 13 + k].to_broadcast([P, P]), ident[:])
            nc.scalar.copy(
                out=rls_n[:].rearrange("p (u q e) -> p u q e", u=2, q=P, e=2),
                in_=pb[:].rearrange("p (u e) q -> p u q e", u=2, e=2),
            )

        def natural_part(n):
            wv = ring.tile([P, D - NAT0], F32, tag="wv", name="wv")
            nc.vector.tensor_tensor(out=wv[:], in0=nat[n][:, NAT0:D], in1=rls_n[:], op=ALU.mult)
            nc.scalar.activation(out=junk2[:], in_=wv[:], func=ACT.Square, accum_out=csq_n[:, n : n + 1])
            nc.scalar.mul(out=nh_n[:, n : n + 1], in_=csq_n[:, n : n + 1], mul=-0.5)

        def squares(n, h):
            sq = ring.tile([P, 8, P], F32, tag="sq", name="sq")
            view = (
                banks[(n, h)][:]
                .rearrange("p u g j -> p (u g j)")
                .bitcast(BF16)
                .rearrange("p (u g j e) -> p u g e j", u=2, g=2, j=P, e=2)
            )
            k = 0
            for gg in range(2 - h):
                for u in range(2):
                    for e in range(2):
                        c = 4 * (2 * h + gg) + 2 * u + e
                        nc.scalar.activation(
                            out=sq[:, k, :], in_=view[:, u, gg, e, :], func=ACT.Square, scale=rls_t[:, c : c + 1]
                        )
                        k += 1
            squared[(n, h)] = sq

        def sum_planes(n):
            rt = ps_r.tile([P, 512], F32, tag="r", name="rt")
            for h in range(2):
                for k in range(8 - 4 * h):
                    nc.tensor.matmul(
                        out=rt[:, 0:P],
                        lhsT=squared[(n, h)][:, k, :],
                        rhs=ident[:],
                        is_transpose=True,
                        start=(h == 0 and k == 0),
                        stop=(h == 1 and k == 3),
                    )
            sums[n] = rt

        def finish_sum(n):
            nc.scalar.activation(out=junk[:], in_=sums[n][:, 0:P], func=ACT.Copy, accum_out=csq_t[:, n : n + 1])
            nc.scalar.activation(
                out=nh[:, n : n + 1], in_=csq_t[:, n : n + 1], func=ACT.Identity, scale=-0.5, bias=nh_n[:, n : n + 1]
            )

        def scale_bank(n, h):
            if h == 0:
                grouped[n] = ring.tile([P, 4, P, 4], BF16, tag="grouped", name="gr", align_bytes=64)
            nc.vector.tensor_tensor(
                out=grouped[n][:, 2 * h : 2 * h + 2, :, :].rearrange("p g j (u e) -> p g j u e", u=2, e=2),
                in0=banks[(n, h)][:]
                .rearrange("p u g j -> p (u g j)")
                .bitcast(BF16)
                .rearrange("p (u g j e) -> p g j u e", u=2, g=2, j=P, e=2),
                in1=rls_t[:, 8 * h : 8 * h + 8]
                .rearrange("p (g u e) -> p g u e", g=2, u=2, e=2)
                .unsqueeze(2)
                .to_broadcast([P, 2, P, 2, 2]),
                op=ALU.mult,
            )

        def quantise(n):
            if n == 0:
                cd, pl = x_codes, x_plane
            else:
                cd = ring.tile([P, 512], U32, tag="codes", name="cd", align_bytes=64, bufs=6)
                pl = ring.tile([P, 512], U8, tag="plane", name="pl", align_bytes=64, bufs=6)
            codes[n] = (cd, pl)
            nc.vector.quantize_mx(
                out=cd[:].bitcast(FP8X4), scales=pl[:], in_=grouped[n][:].rearrange("p g j t -> p (g j t)")
            )

        def stage1(n):
            g, t = (n - 1) // 4, (n - 1) % 4
            if t == 0:
                z_bank[g] = ps_z.tile([P, 4, P], F32, tag="z", name="zb")
            cd, pl = codes[n]
            for c in range(4):
                cols = slice(P * c, P * c + P)
                nc.tensor.matmul_mx(
                    out=z_bank[g][:, t, :],
                    lhsT=cd[:, cols].bitcast(FP8X4),
                    lhsT_scale=pl[:, cols],
                    rhs=x_codes[:, cols].bitcast(FP8X4),
                    rhs_scale=x_plane[:, cols],
                    start=(c == 0),
                    stop=(c == 3),
                )

        def exponent(g, t0, t1):
            if t0 == 0:
                z1s[g] = work.tile([P, 4, P], F32, tag="z1", name="z1")
                exps[g] = work.tile([P, 4, P], F32, tag="ex", name="ex")
            nc.vector.tensor_tensor(
                out=z1s[g][:, t0:t1, :],
                in0=z_bank[g][:, t0:t1, :],
                in1=nhx_b[:].unsqueeze(1).to_broadcast([P, t1 - t0, P]),
                op=ALU.add,
            )
            for t in range(t0, t1):
                n = 4 * g + t + 1
                nc.scalar.activation(
                    out=exps[g][:, t, :], in_=z1s[g][:, t, :], func=ACT.Exp, bias=nh[:, n : n + 1], scale=1.0
                )

        def clamp(g):
            kg = work.tile([P, P, 4], BF16, tag="kg", name="kg", align_bytes=64)
            view = exps[g][:].rearrange("p t i -> p i t")
            nc.vector.tensor_scalar(out=kg[:], in0=view, scalar1=1.0, scalar2=None, op0=ALU.min)
            kgs[g] = kg

        def quantise_k(g):
            nc.vector.quantize_mx(
                out=k_codes[g][:].bitcast(FP8X4), scales=k_plane[g][:], in_=kgs[g][:].rearrange("p i t -> p (i t)")
            )

        accs = []

        def stage2(g, c):
            nc.tensor.matmul_mx(
                out=accs[c][:],
                lhsT=k_codes[g][:].bitcast(FP8X4),
                lhsT_scale=k_plane[g][:],
                rhs=w_words[g][:, 2048 * c : 2048 * c + 2048].bitcast(FP8X4),
                rhs_scale=planes[4 * g : P, 512 * c : 512 * c + 512],
                start=(g == 0),
                stop=(g == 3),
            )

        transposes(0)
        spread_rls()
        for s in range(TILES):
            if s == 3:
                nc.vector.tensor_copy(out=nhx_b[:], in_=banks["xsq"][:, 0:P])
            if s >= 1:
                sum_planes(s - 1)
            if s == 16:
                sum_planes(16)
            if s + 1 < TILES:
                transposes(s + 1)
            scale_bank(s, 0)
            if s < 16:
                squares(s, 0)
            if s >= 1:
                finish_sum(s - 1)
            scale_bank(s, 1)
            if s < 16:
                squares(s, 1)
            natural_part(s)
            if s == 15:
                squares(16, 0)
                squares(16, 1)
            if s == 16:
                finish_sum(16)
                exponent(3, 0, 2)
            if s >= 1:
                quantise(s - 1)
            if s >= 5 and s % 4 == 1 and s < 15:
                for n in range(s - 4, s):
                    stage1(n)
            if s == 15:
                stage1(13)
                stage1(14)
            if s == 16:
                stage1(15)
            if s == 1:
                pm = ps_r.tile([P, 512], F32, tag="r", name="pm")
                nc.tensor.transpose(pm[:, 0:P], nh[:, 0:1].to_broadcast([P, P]), ident[:])
                banks["xsq"] = pm
            if s == 15:
                for c in range(2):
                    acc = ps_t.tile([P, 512], F32, tag="t", name="acc")
                    accs.append(acc)
                    stage2(0, c)
                    stage2(1, c)
            if s >= 6 and s % 4 == 2 and s < 16:
                exponent((s - 6) // 4, 0, 4)
            if s >= 7 and s % 4 == 3:
                clamp((s - 7) // 4)
            if s >= 8 and s % 4 == 0:
                quantise_k((s - 8) // 4)

        quantise(16)
        stage1(16)
        stage2(2, 0)
        stage2(2, 1)
        for c in range(2, 4):
            acc = ps_t.tile([P, 512], F32, tag="t", name="acc")
            accs.append(acc)
            for g in range(3):
                stage2(g, c)
        exponent(3, 2, 4)
        clamp(3)
        quantise_k(3)
        out_rows = out.rearrange("b l n -> (b l) n")
        for c in range(4):
            stage2(3, c)
            res = work.tile([P, 512], F32, tag="res", name="res", bufs=4)
            cols = slice(512 * c, 512 * c + 512)
            nc.vector.tensor_tensor(out=res[:], in0=accs[c][:], in1=bias_b[:, cols], op=ALU.add)
            nc.sync.dma_start(out=out_rows[:, cols], in_=res[:])
